import numpy as np
import ml_dtypes


def mxq(x, axis, fmt="e4m3"):
    dtype, down = {"e4m3": (ml_dtypes.float8_e4m3fn, 7), "e5m2": (ml_dtypes.float8_e5m2, 14)}[fmt]
    v = np.moveaxis(np.asarray(x, np.float32).astype(ml_dtypes.bfloat16).astype(np.float64), axis, -1)
    blocks = v.reshape(v.shape[:-1] + (-1, 32))
    amax = np.abs(blocks).max(-1, keepdims=True)
    byte = np.maximum(np.where(amax > 0, np.frexp(amax)[1] - 1 + 127, 0) - down, 1)
    scale = np.exp2(byte - 127.0)
    codes = (blocks / scale).astype(np.float32).astype(dtype).astype(np.float64)
    return np.moveaxis((codes * scale).reshape(v.shape), -1, axis)


WIDE = False


def mx_kscale(k):
    if not WIDE:
        return np.ones(k)
    levels = np.array([30, -30])
    if k % 512:
        return np.exp2(np.random.permutation(np.resize(levels, k // 32))).repeat(32)
    a = np.empty((k // 512, 16))
    for p in range(k // 512):
        a[p, :8] = np.random.permutation(np.resize(levels, 8))
        for g in range(8):
            far = levels[np.abs(levels - a[p, g]) >= 10]
            a[p, g + 8] = far[np.random.randint(len(far))]
    return np.exp2(a.ravel()).repeat(32)


BF16 = ml_dtypes.bfloat16


def bf(x):
    return np.asarray(x, np.float32).astype(BF16)


def f64(x):
    return np.asarray(x).astype(np.float64)


B, SEQ, DIM, N_HEADS, N_KV, HEAD, HIDDEN = 1, 512, 2048, 16, 4, 128, 5504
ROPE_THETA = 10000.0
HALF = HEAD // 2


def rope(t, cos, sin):
    t2 = t.reshape(*t.shape[:-1], HALF, 2)
    t0, t1 = t2[..., 0], t2[..., 1]
    c = cos[None, :, None, :]
    s = sin[None, :, None, :]
    out = np.stack([t0 * c - t1 * s, t0 * s + t1 * c], axis=-1)
    return out.reshape(t.shape)


def setup_inputs():
    s = mx_kscale(DIM)
    inv = 1.0 / (ROPE_THETA ** (np.arange(0, HEAD, 2) / HEAD))
    freqs = np.outer(np.arange(SEQ), inv)
    return {"x": bf(np.random.standard_normal((B, SEQ, DIM)) * s),
            "freqs_cos": bf(np.cos(freqs)),
            "freqs_sin": bf(np.sin(freqs)),
            "wq": bf(np.random.standard_normal((DIM, N_HEADS * HEAD)) * 1.25 / np.sqrt(DIM) / s[:, None]),
            "wk": bf(np.random.standard_normal((DIM, N_KV * HEAD)) * 1.25 / np.sqrt(DIM) / s[:, None]),
            "wv": bf(np.random.standard_normal((DIM, N_KV * HEAD)) * 1.5 / np.sqrt(DIM) / s[:, None])}


def reference(x, freqs_cos, freqs_sin, wq, wk, wv):
    xm = mxq(f64(x).reshape(B * SEQ, DIM), 1, "e5m2")
    q = (xm @ mxq(f64(wq), 0, "e5m2")).reshape(B, SEQ, N_HEADS, HEAD)
    k = (xm @ mxq(f64(wk), 0, "e5m2")).reshape(B, SEQ, N_KV, HEAD)
    v = (xm @ mxq(f64(wv), 0, "e5m2")).reshape(B, SEQ, N_KV, HEAD)
    c, s = f64(freqs_cos), f64(freqs_sin)
    return rope(q, c, s), rope(k, c, s), v

@@ -1,0 +1,285 @@
+from contextlib import ExitStack
+
+import concourse.mybir as mybir
+from concourse.masks import make_identity
+
+F32 = mybir.dt.float32
+BF16 = mybir.dt.bfloat16
+U32 = mybir.dt.uint32
+U8 = mybir.dt.uint8
+FP8X4 = mybir.dt.float8_e5m2_x4
+MULT = mybir.AluOpType.mult
+ADD = mybir.AluOpType.add
+
+P = 128
+PACK = 4
+K = 2048
+K_PASS = P * PACK
+PASSES = K // K_PASS
+TOKENS = 512
+TOKEN_TILES = TOKENS // P
+N_TILE = 512
+GROUPS = 6
+UNITS = GROUPS * PASSES
+HEADS_PER_GROUP = 4
+HALF = 64
+RUN = 4
+
+FLOPS = 2 * TOKENS * K * (GROUPS * N_TILE)
+
+LOOK = 3
+SPLIT = 280
+HEAD_VECTOR_UNITS = (0, 2, 3, 5)
+USE_GPSIMD = True
+
+
+def scalar_columns(u):
+    if u in HEAD_VECTOR_UNITS:
+        return 0
+    if u >= 7 and u % PASSES == PASSES - 1:
+        return SPLIT
+    return N_TILE
+
+
+def tile_transformerblock_pa_kernel(tc, x, freqs_cos, freqs_sin, wq, wk, wv, out_0, out_1, out_2):
+    nc = tc.nc
+    x_rows = x.flatten_outer_dims()
+    q_out = out_0.rearrange("b s h d -> (b s) (h d)")
+    k_out = out_1.rearrange("b s h d -> (b s) (h d)")
+    v_out = out_2.rearrange("b s h d -> (b s) (h d)")
+    o_of = [(q_out, 0), (q_out, 512), (q_out, 1024), (q_out, 1536), (k_out, 0), (v_out, 0)]
+
+    with ExitStack() as ctx:
+        const = ctx.enter_context(tc.tile_pool(name="const", bufs=1))
+        wg_pool = ctx.enter_context(tc.tile_pool(name="wg", bufs=7))
+        xg_pool = ctx.enter_context(tc.tile_pool(name="xg", bufs=2))
+        wc_pool = ctx.enter_context(tc.tile_pool(name="wc", bufs=3))
+        res_pool = ctx.enter_context(tc.tile_pool(name="res", bufs=12))
+        rot_pool = ctx.enter_context(tc.tile_pool(name="rot", bufs=4))
+        psum = ctx.enter_context(tc.psum_pool(name="psum", bufs=8))
+        ctx.enter_context(tc.manual_schedule())
+
+        cos_sb = const.tile([P, TOKEN_TILES, HALF, 1], BF16, name="cos_sb", tag="cos_sb")
+        sin_sb = const.tile([P, TOKEN_TILES, HALF, 1], BF16, name="sin_sb", tag="sin_sb")
+        nc.scalar.dma_start(
+            out=sin_sb[:].rearrange("p t i o -> p t (i o)"),
+            in_=freqs_sin.rearrange("(t p) i -> p t i", p=P),
+        )
+        nc.scalar.dma_start(
+            out=cos_sb[:].rearrange("p t i o -> p t (i o)"),
+            in_=freqs_cos.rearrange("(t p) i -> p t i", p=P),
+        )
+
+        raw = {}
+        x_sb = []
+
+        def load_w(w, g, c0, width, first_group):
+            t = const.tile([P, PACK, width], BF16, name="raw%d_%d" % (first_group, g), tag="raw%d_%d" % (first_group, g))
+            nc.sync.dma_start(
+                out=t[:],
+                in_=w[g * K_PASS : (g + 1) * K_PASS, c0 : c0 + width].rearrange("(p j) c -> p j c", j=PACK),
+            )
+            for n in range(width // N_TILE):
+                raw[(first_group + n) * PASSES + g] = t[:, :, n * N_TILE : (n + 1) * N_TILE]
+
+        def load_x(mt):
+            t = const.tile([P, K], BF16, name="x_sb%d" % mt, tag="x_sb%d" % mt)
+            nc.sync.dma_start(out=t[:], in_=x_rows[mt * P : (mt + 1) * P, :])
+            x_sb.append(t)
+
+        for g in range(PASSES):
+            load_w(wq, g, 0, N_TILE, 0)
+        load_w(wq, 0, N_TILE, N_TILE, 1)
+        load_w(wq, 1, N_TILE, N_TILE, 1)
+        for mt in range(TOKEN_TILES):
+            load_x(mt)
+        load_w(wq, 2, N_TILE, N_TILE, 1)
+        load_w(wq, 3, N_TILE, N_TILE, 1)
+        for g in range(PASSES):
+            load_w(wq, g, 2 * N_TILE, 2 * N_TILE, 2)
+        for g in range(PASSES):
+            load_w(wk, g, 0, N_TILE, 4)
+        for g in range(PASSES):
+            load_w(wv, g, 0, N_TILE, 5)
+
+        ident = const.tile([P, P], F32, name="ident", tag="ident")
+        make_identity(nc, ident[:])
+
+        sin_pm = const.tile([P, TOKEN_TILES, HALF, 2], BF16, name="sin_pm", tag="sin_pm")
+        nc.vector.tensor_scalar_mul(out=sin_pm[:, :, :, 0:1], in0=sin_sb[:], scalar1=-1.0)
+        nc.vector.tensor_copy(out=sin_pm[:, :, :, 1:2], in_=sin_sb[:])
+
+        x_codes = const.tile([P, TOKEN_TILES, PASSES, P], U32, name="x_codes", tag="x_codes", align_bytes=64)
+        x_scales = const.tile([P, TOKEN_TILES, PASSES, P], U8, name="x_scales", tag="x_scales", align_bytes=64)
+
+        grouped = {}
+        codes = {}
+        banks = {}
+        x_banks = {}
+        x_grouped = {}
+        sums = {}
+        issued = [0]
+
+        def interleave(u):
+            t = wg_pool.tile([P, N_TILE, PACK], BF16, name="wgrp", tag="wgrp", align_bytes=64)
+            grouped[u] = t
+            cut = scalar_columns(u)
+            if cut > 0:
+                nc.scalar.copy(
+                    out=t[:, 0:cut, :].rearrange("p (c i) j -> p c j i", i=RUN),
+                    in_=raw[u][:, :, 0:cut].rearrange("p j (c i) -> p c j i", i=RUN),
+                )
+            if cut < N_TILE:
+                nc.vector.tensor_copy(
+                    out=t[:, cut:N_TILE, :].rearrange("p (c i) j -> p c j i", i=RUN),
+                    in_=raw[u][:, :, cut:N_TILE].rearrange("p j (c i) -> p c j i", i=RUN),
+                )
+
+        def interleave_up_to(u):
+            while issued[0] <= min(u, UNITS - 1):
+                interleave(issued[0])
+                issued[0] += 1
+
+        def quantize(u):
+            ng, g = divmod(u, PASSES)
+            if g == 0:
+                wc = wc_pool.tile([P, PASSES, N_TILE], U32, name="wcodes", tag="wcodes", align_bytes=64)
+                ws = wc_pool.tile([P, PASSES, N_TILE], U8, name="wscales", tag="wscales", align_bytes=64)
+                codes[ng] = (wc, ws)
+            wc, ws = codes[ng]
+            nc.vector.quantize_mx(
+                out=wc[:, g, :].bitcast(FP8X4),
+                scales=ws[:, g, :],
+                in_=grouped[u][:].rearrange("p c j -> p (c j)"),
+            )
+
+        def multiply(u, token_tiles):
+            ng, g = divmod(u, PASSES)
+            wc, ws = codes[ng]
+            for mt in token_tiles:
+                if g == 0:
+                    acc = psum.tile([P, N_TILE], F32, name="bank", tag="bank")
+                    banks[(ng, mt)] = acc
+                acc = banks[(ng, mt)]
+                nc.tensor.matmul_mx(
+                    out=acc[:],
+                    lhsT=x_codes[:, mt, g, :].bitcast(FP8X4),
+                    lhsT_scale=x_scales[:, mt, g, :],
+                    rhs=wc[:, g, :].bitcast(FP8X4),
+                    rhs_scale=ws[:, g, :],
+                    start=(g == 0),
+                    stop=(g == PASSES - 1),
+                )
+
+        def transpose_x(mt):
+            words = x_sb[mt][:].bitcast(F32)
+            for half in range(2):
+                xt = psum.tile([P, 2, 2, P], F32, name="bank", tag="bank")
+                x_banks[(mt, half)] = xt
+                for gl in range(2):
+                    g = 2 * half + gl
+                    for s in range(2):
+                        nc.tensor.transpose(
+                            xt[:, gl, s, :], words[:, 256 * g + s : 256 * (g + 1) : 2], ident[:]
+                        )
+
+        def gather_x(mt):
+            xg = xg_pool.tile([P, PASSES, P, PACK], BF16, name="xgrp", tag="xgrp", align_bytes=64)
+            x_grouped[mt] = xg
+            for half in range(2):
+                nc.scalar.copy(
+                    out=xg[:, 2 * half : 2 * half + 2, :, :].bitcast(F32),
+                    in_=x_banks[(mt, half)][:].rearrange("p g s t -> p g t s"),
+                )
+
+        def quantize_x(mt):
+            nc.vector.quantize_mx(
+                out=x_codes[:, mt, :, :].rearrange("p g t -> p (g t)").bitcast(FP8X4),
+                scales=x_scales[:, mt, :, :].rearrange("p g t -> p (g t)"),
+                in_=x_grouped[mt][:].rearrange("p g t j -> p (g t j)"),
+            )
+
+        def store(ng, mt, res):
+            o_ap, c0 = o_of[ng]
+            nc.sync.dma_start(out=o_ap[mt * P : (mt + 1) * P, c0 : c0 + N_TILE], in_=res[:])
+
+        def rotate(ng, mt):
+            acc = banks[(ng, mt)]
+            res = res_pool.tile([P, N_TILE], F32, name="res", tag="res")
+            rot = rot_pool.tile([P, N_TILE], F32, name="rot", tag="rot")
+            sums[(ng, mt)] = (res, rot)
+            pairs = acc[:].rearrange("p (h i e) -> p h i e", h=HEADS_PER_GROUP, e=2)
+            shape = [P, HEADS_PER_GROUP, HALF, 2]
+            nc.vector.tensor_tensor(
+                out=res[:].rearrange("p (h i e) -> p h i e", h=HEADS_PER_GROUP, e=2),
+                in0=pairs,
+                in1=cos_sb[:, mt : mt + 1, :, :].to_broadcast(shape),
+                op=MULT,
+            )
+            nc.vector.tensor_tensor(
+                out=rot[:].rearrange("p (h i e) -> p h i e", h=HEADS_PER_GROUP, e=2),
+                in0=pairs[:, :, :, ::-1],
+                in1=sin_pm[:, mt : mt + 1, :, :].to_broadcast(shape),
+                op=MULT,
+            )
+
+        def add_and_store(ng, mt, engine):
+            res, rot = sums[(ng, mt)]
+            engine.tensor_tensor(out=res[:], in0=res[:], in1=rot[:], op=ADD)
+            store(ng, mt, res)
+
+        def copy_and_store(mt):
+            res = res_pool.tile([P, N_TILE], F32, name="res", tag="res")
+            nc.scalar.copy(out=res[:], in_=banks[(GROUPS - 1, mt)][:])
+            store(GROUPS - 1, mt, res)
+
+        helper = nc.gpsimd if USE_GPSIMD else nc.vector
+
+        def rope_run(ng, token_tiles):
+            for n, mt in enumerate(token_tiles):
+                rotate(ng, mt)
+                if n > 0:
+                    add_and_store(ng, token_tiles[n - 1], helper)
+
+        all_tiles = list(range(TOKEN_TILES))
+
+        interleave_up_to(1)
+        quantize(0)
+        interleave_up_to(3)
+        quantize(1)
+        interleave_up_to(4)
+        quantize(2)
+        quantize(3)
+        interleave_up_to(5)
+        for mt in all_tiles:
+            transpose_x(mt)
+        for mt in all_tiles:
+            gather_x(mt)
+            if mt < 2:
+                quantize(4 + mt)
+            quantize_x(mt)
+            for g in range(PASSES):
+                multiply(g, [mt])
+        multiply(4, all_tiles)
+        multiply(5, all_tiles)
+        interleave_up_to(6)
+
+        for c in range(GROUPS - 2):
+            rope_run(c, all_tiles)
+            interleave_up_to(PASSES * (c + 2) + 1 + LOOK)
+            add_and_store(c, TOKEN_TILES - 1, nc.vector)
+            for u in range(PASSES * (c + 1) + 2, PASSES * (c + 2) + 2):
+                if u >= 6:
+                    quantize(u)
+                    multiply(u, all_tiles)
+
+        last = GROUPS - 2
+        rope_run(last, [0, 1])
+        add_and_store(last, 1, nc.vector)
+        for u in (UNITS - 2, UNITS - 1):
+            quantize(u)
+            multiply(u, all_tiles)
+        for mt in all_tiles:
+            copy_and_store(mt)
+        rope_run(last, [2, 3])
+        add_and_store(last, 3, nc.vector)

@@ -30,7 +30,7 @@ FLOPS = 2 * TOKENS * K * (GROUPS * N_TILE)
 LOOK = 3
 SPLIT = 280
 HEAD_VECTOR_UNITS = (0, 2, 3, 5)
-USE_GPSIMD = True
+USE_GPSIMD = False
 
 
 def scalar_columns(u):

@@ -23,14 +23,13 @@ GROUPS = 6
 UNITS = GROUPS * PASSES
 HEADS_PER_GROUP = 4
 HALF = 64
-RUN = 4
 
 FLOPS = 2 * TOKENS * K * (GROUPS * N_TILE)
 
 LOOK = 3
 SPLIT = 280
 HEAD_VECTOR_UNITS = (0, 2, 3, 5)
-USE_GPSIMD = False
+USE_GPSIMD = True
 
 
 def scalar_columns(u):
@@ -126,13 +125,13 @@ def tile_transformerblock_pa_kernel(tc, x, freqs_cos, freqs_sin, wq, wk, wv, out
             cut = scalar_columns(u)
             if cut > 0:
                 nc.scalar.copy(
-                    out=t[:, 0:cut, :].rearrange("p (c i) j -> p c j i", i=RUN),
-                    in_=raw[u][:, :, 0:cut].rearrange("p j (c i) -> p c j i", i=RUN),
+                    out=t[:, 0:cut, :],
+                    in_=raw[u][:, :, 0:cut].rearrange("p j c -> p c j"),
                 )
             if cut < N_TILE:
                 nc.vector.tensor_copy(
-                    out=t[:, cut:N_TILE, :].rearrange("p (c i) j -> p c j i", i=RUN),
-                    in_=raw[u][:, :, cut:N_TILE].rearrange("p j (c i) -> p c j i", i=RUN),
+                    out=t[:, cut:N_TILE, :],
+                    in_=raw[u][:, :, cut:N_TILE].rearrange("p j c -> p c j"),
                 )
 
         def interleave_up_to(u):

@@ -23,11 +23,12 @@ GROUPS = 6
 UNITS = GROUPS * PASSES
 HEADS_PER_GROUP = 4
 HALF = 64
+RUN = 4
 
 FLOPS = 2 * TOKENS * K * (GROUPS * N_TILE)
 
 LOOK = 3
-SPLIT = 280
+SPLIT = 0
 HEAD_VECTOR_UNITS = (0, 2, 3, 5)
 USE_GPSIMD = True
 
@@ -125,13 +126,13 @@ def tile_transformerblock_pa_kernel(tc, x, freqs_cos, freqs_sin, wq, wk, wv, out
             cut = scalar_columns(u)
             if cut > 0:
                 nc.scalar.copy(
-                    out=t[:, 0:cut, :],
-                    in_=raw[u][:, :, 0:cut].rearrange("p j c -> p c j"),
+                    out=t[:, 0:cut, :].rearrange("p (c i) j -> p c j i", i=RUN),
+                    in_=raw[u][:, :, 0:cut].rearrange("p j (c i) -> p c j i", i=RUN),
                 )
             if cut < N_TILE:
                 nc.vector.tensor_copy(
-                    out=t[:, cut:N_TILE, :],
-                    in_=raw[u][:, :, cut:N_TILE].rearrange("p j c -> p c j"),
+                    out=t[:, cut:N_TILE, :].rearrange("p (c i) j -> p c j i", i=RUN),
+                    in_=raw[u][:, :, cut:N_TILE].rearrange("p j (c i) -> p c j i", i=RUN),
                 )
 
         def interleave_up_to(u):

@@ -23,14 +23,13 @@ GROUPS = 6
 UNITS = GROUPS * PASSES
 HEADS_PER_GROUP = 4
 HALF = 64
-RUN = 4
 
 FLOPS = 2 * TOKENS * K * (GROUPS * N_TILE)
 
 LOOK = 3
-SPLIT = 0
-HEAD_VECTOR_UNITS = (0, 2, 3, 5)
-USE_GPSIMD = True
+SPLIT = 304
+HEAD_VECTOR_UNITS = (0, 1, 3, 5, 6)
+GPSIMD_ADDS = 2
 
 
 def scalar_columns(u):
@@ -71,7 +70,7 @@ def tile_transformerblock_pa_kernel(tc, x, freqs_cos, freqs_sin, wq, wk, wv, out
         )
 
         raw = {}
-        x_sb = []
+        x_sb = {}
 
         def load_w(w, g, c0, width, first_group):
             t = const.tile([P, PACK, width], BF16, name="raw%d_%d" % (first_group, g), tag="raw%d_%d" % (first_group, g))
@@ -85,14 +84,18 @@ def tile_transformerblock_pa_kernel(tc, x, freqs_cos, freqs_sin, wq, wk, wv, out
         def load_x(mt):
             t = const.tile([P, K], BF16, name="x_sb%d" % mt, tag="x_sb%d" % mt)
             nc.sync.dma_start(out=t[:], in_=x_rows[mt * P : (mt + 1) * P, :])
-            x_sb.append(t)
+            x_sb[mt] = t
 
-        for g in range(PASSES):
-            load_w(wq, g, 0, N_TILE, 0)
+        load_w(wq, 0, 0, N_TILE, 0)
+        load_w(wq, 1, 0, N_TILE, 0)
+        load_w(wq, 2, 0, N_TILE, 0)
+        load_x(0)
+        load_w(wq, 3, 0, N_TILE, 0)
         load_w(wq, 0, N_TILE, N_TILE, 1)
+        load_x(1)
+        load_x(2)
         load_w(wq, 1, N_TILE, N_TILE, 1)
-        for mt in range(TOKEN_TILES):
-            load_x(mt)
+        load_x(3)
         load_w(wq, 2, N_TILE, N_TILE, 1)
         load_w(wq, 3, N_TILE, N_TILE, 1)
         for g in range(PASSES):
@@ -125,14 +128,10 @@ def tile_transformerblock_pa_kernel(tc, x, freqs_cos, freqs_sin, wq, wk, wv, out
             grouped[u] = t
             cut = scalar_columns(u)
             if cut > 0:
-                nc.scalar.copy(
-                    out=t[:, 0:cut, :].rearrange("p (c i) j -> p c j i", i=RUN),
-                    in_=raw[u][:, :, 0:cut].rearrange("p j (c i) -> p c j i", i=RUN),
-                )
+                nc.scalar.copy(out=t[:, 0:cut, :], in_=raw[u][:, :, 0:cut].rearrange("p j c -> p c j"))
             if cut < N_TILE:
                 nc.vector.tensor_copy(
-                    out=t[:, cut:N_TILE, :].rearrange("p (c i) j -> p c j i", i=RUN),
-                    in_=raw[u][:, :, cut:N_TILE].rearrange("p j (c i) -> p c j i", i=RUN),
+                    out=t[:, cut:N_TILE, :], in_=raw[u][:, :, cut:N_TILE].rearrange("p j c -> p c j")
                 )
 
         def interleave_up_to(u):
@@ -233,53 +232,63 @@ def tile_transformerblock_pa_kernel(tc, x, freqs_cos, freqs_sin, wq, wk, wv, out
             nc.scalar.copy(out=res[:], in_=banks[(GROUPS - 1, mt)][:])
             store(GROUPS - 1, mt, res)
 
-        helper = nc.gpsimd if USE_GPSIMD else nc.vector
-
-        def rope_run(ng, token_tiles):
-            for n, mt in enumerate(token_tiles):
-                rotate(ng, mt)
-                if n > 0:
-                    add_and_store(ng, token_tiles[n - 1], helper)
-
         all_tiles = list(range(TOKEN_TILES))
 
-        interleave_up_to(1)
+        def quantize_and_multiply(u):
+            quantize(u)
+            multiply(u, all_tiles)
+
+        interleave_up_to(2)
+        for mt in all_tiles:
+            transpose_x(mt)
         quantize(0)
-        interleave_up_to(3)
         quantize(1)
+        gather_x(0)
         interleave_up_to(4)
         quantize(2)
         quantize(3)
+        quantize_x(0)
+        quantize(4)
+        gather_x(1)
         interleave_up_to(5)
+        quantize_x(1)
+        gather_x(2)
+        quantize_x(2)
+        interleave_up_to(6)
+        gather_x(3)
+        quantize_x(3)
+        quantize(5)
         for mt in all_tiles:
-            transpose_x(mt)
-        for mt in all_tiles:
-            gather_x(mt)
-            if mt < 2:
-                quantize(4 + mt)
-            quantize_x(mt)
             for g in range(PASSES):
                 multiply(g, [mt])
         multiply(4, all_tiles)
         multiply(5, all_tiles)
-        interleave_up_to(6)
 
         for c in range(GROUPS - 2):
-            rope_run(c, all_tiles)
-            interleave_up_to(PASSES * (c + 2) + 1 + LOOK)
-            add_and_store(c, TOKEN_TILES - 1, nc.vector)
-            for u in range(PASSES * (c + 1) + 2, PASSES * (c + 2) + 2):
-                if u >= 6:
-                    quantize(u)
-                    multiply(u, all_tiles)
+            for mt in all_tiles:
+                rotate(c, mt)
+                if 0 < mt <= GPSIMD_ADDS:
+                    add_and_store(c, mt - 1, nc.gpsimd)
+            first = PASSES * (c + 1) + 2
+            interleave_up_to(first + 1)
+            quantize_and_multiply(first)
+            quantize_and_multiply(first + 1)
+            interleave_up_to(first + 3 + LOOK)
+            for mt in range(GPSIMD_ADDS, TOKEN_TILES):
+                add_and_store(c, mt, nc.vector)
+            quantize_and_multiply(first + 2)
+            quantize_and_multiply(first + 3)
 
         last = GROUPS - 2
-        rope_run(last, [0, 1])
+        rotate(last, 0)
+        rotate(last, 1)
+        add_and_store(last, 0, nc.gpsimd)
+        quantize_and_multiply(UNITS - 2)
         add_and_store(last, 1, nc.vector)
-        for u in (UNITS - 2, UNITS - 1):
-            quantize(u)
-            multiply(u, all_tiles)
+        quantize_and_multiply(UNITS - 1)
         for mt in all_tiles:
             copy_and_store(mt)
-        rope_run(last, [2, 3])
+        rotate(last, 2)
+        rotate(last, 3)
+        add_and_store(last, 2, nc.vector)
         add_and_store(last, 3, nc.vector)

@@ -53,8 +53,8 @@ def tile_transformerblock_pa_kernel(tc, x, freqs_cos, freqs_sin, wq, wk, wv, out
         wg_pool = ctx.enter_context(tc.tile_pool(name="wg", bufs=7))
         xg_pool = ctx.enter_context(tc.tile_pool(name="xg", bufs=2))
         wc_pool = ctx.enter_context(tc.tile_pool(name="wc", bufs=3))
-        res_pool = ctx.enter_context(tc.tile_pool(name="res", bufs=12))
-        rot_pool = ctx.enter_context(tc.tile_pool(name="rot", bufs=4))
+        res_pool = ctx.enter_context(tc.tile_pool(name="res", bufs=6))
+        prod_pool = ctx.enter_context(tc.tile_pool(name="prod", bufs=2))
         psum = ctx.enter_context(tc.psum_pool(name="psum", bufs=8))
         ctx.enter_context(tc.manual_schedule())
 
@@ -108,9 +108,12 @@ def tile_transformerblock_pa_kernel(tc, x, freqs_cos, freqs_sin, wq, wk, wv, out
         ident = const.tile([P, P], F32, name="ident", tag="ident")
         make_identity(nc, ident[:])
 
-        sin_pm = const.tile([P, TOKEN_TILES, HALF, 2], BF16, name="sin_pm", tag="sin_pm")
-        nc.vector.tensor_scalar_mul(out=sin_pm[:, :, :, 0:1], in0=sin_sb[:], scalar1=-1.0)
-        nc.vector.tensor_copy(out=sin_pm[:, :, :, 1:2], in_=sin_sb[:])
+        table = const.tile([P, TOKEN_TILES, 2 * HALF, 2], BF16, name="table", tag="table")
+        by_pair = table[:].rearrange("p t (i a) b -> p t i (a b)", a=2)
+        nc.vector.tensor_copy(out=by_pair[:, :, :, 0:1], in_=cos_sb[:])
+        nc.vector.tensor_copy(out=by_pair[:, :, :, 1:2], in_=sin_sb[:])
+        nc.vector.tensor_scalar_mul(out=by_pair[:, :, :, 2:3], in0=sin_sb[:], scalar1=-1.0)
+        nc.vector.tensor_copy(out=by_pair[:, :, :, 3:4], in_=cos_sb[:])
 
         x_codes = const.tile([P, TOKEN_TILES, PASSES, P], U32, name="x_codes", tag="x_codes", align_bytes=64)
         x_scales = const.tile([P, TOKEN_TILES, PASSES, P], U8, name="x_scales", tag="x_scales", align_bytes=64)
@@ -121,6 +124,7 @@ def tile_transformerblock_pa_kernel(tc, x, freqs_cos, freqs_sin, wq, wk, wv, out
         x_banks = {}
         x_grouped = {}
         sums = {}
+        prods = {}
         issued = [0]
 
         def interleave(u):
@@ -157,11 +161,11 @@ def tile_transformerblock_pa_kernel(tc, x, freqs_cos, freqs_sin, wq, wk, wv, out
             wc, ws = codes[ng]
             for mt in token_tiles:
                 if g == 0:
-                    acc = psum.tile([P, N_TILE], F32, name="bank", tag="bank")
+                    acc = psum.tile([P, HEADS_PER_GROUP, 2 * HALF, 1], F32, name="bank", tag="bank")
                     banks[(ng, mt)] = acc
                 acc = banks[(ng, mt)]
                 nc.tensor.matmul_mx(
-                    out=acc[:],
+                    out=acc[:].rearrange("p h c o -> p (h c o)"),
                     lhsT=x_codes[:, mt, g, :].bitcast(FP8X4),
                     lhsT_scale=x_scales[:, mt, g, :],
                     rhs=wc[:, g, :].bitcast(FP8X4),
@@ -200,37 +204,55 @@ def tile_transformerblock_pa_kernel(tc, x, freqs_cos, freqs_sin, wq, wk, wv, out
 
         def store(ng, mt, res):
             o_ap, c0 = o_of[ng]
-            nc.sync.dma_start(out=o_ap[mt * P : (mt + 1) * P, c0 : c0 + N_TILE], in_=res[:])
+            nc.sync.dma_start(out=o_ap[mt * P : (mt + 1) * P, c0 : c0 + N_TILE], in_=res)
 
         def rotate(ng, mt):
-            acc = banks[(ng, mt)]
-            res = res_pool.tile([P, N_TILE], F32, name="res", tag="res")
-            rot = rot_pool.tile([P, N_TILE], F32, name="rot", tag="rot")
-            sums[(ng, mt)] = (res, rot)
-            pairs = acc[:].rearrange("p (h i e) -> p h i e", h=HEADS_PER_GROUP, e=2)
-            shape = [P, HEADS_PER_GROUP, HALF, 2]
+            if mt % 2 == 0:
+                prods[(ng, mt // 2)] = prod_pool.tile(
+                    [P, 2, HEADS_PER_GROUP, 2 * HALF, 2], F32, name="prod", tag="prod"
+                )
+            shape = [P, HEADS_PER_GROUP, 2 * HALF, 2]
             nc.vector.tensor_tensor(
-                out=res[:].rearrange("p (h i e) -> p h i e", h=HEADS_PER_GROUP, e=2),
-                in0=pairs,
-                in1=cos_sb[:, mt : mt + 1, :, :].to_broadcast(shape),
+                out=prods[(ng, mt // 2)][:, mt % 2, :, :, :],
+                in0=banks[(ng, mt)][:].to_broadcast(shape),
+                in1=table[:, mt : mt + 1, :, :].to_broadcast(shape),
                 op=MULT,
             )
-            nc.vector.tensor_tensor(
-                out=rot[:].rearrange("p (h i e) -> p h i e", h=HEADS_PER_GROUP, e=2),
-                in0=pairs[:, :, :, ::-1],
-                in1=sin_pm[:, mt : mt + 1, :, :].to_broadcast(shape),
-                op=MULT,
-            )
+
+        def result_tile(ng, mt):
+            if mt % 2 == 0:
+                sums[(ng, mt // 2)] = res_pool.tile([P, 2, N_TILE], F32, name="res", tag="res")
+            return sums[(ng, mt // 2)]
 
         def add_and_store(ng, mt, engine):
-            res, rot = sums[(ng, mt)]
-            engine.tensor_tensor(out=res[:], in0=res[:], in1=rot[:], op=ADD)
-            store(ng, mt, res)
+            res = result_tile(ng, mt)
+            terms = prods[(ng, mt // 2)][:, mt % 2, :, :, :].rearrange("p h (i a) b -> p (h i) a b", a=2)
+            engine.tensor_tensor(
+                out=res[:, mt % 2, :].rearrange("p (n b) -> p n b", b=2),
+                in0=terms[:, :, 0, :],
+                in1=terms[:, :, 1, :],
+                op=ADD,
+            )
+            store(ng, mt, res[:, mt % 2, :])
+
+        def add_pair_and_store(ng, half):
+            res = result_tile(ng, 2 * half)
+            terms = prods[(ng, half)][:].rearrange("p t h (i a) b -> p (t h i) a b", a=2)
+            nc.vector.tensor_tensor(
+                out=res[:].rearrange("p t (n b) -> p (t n) b", b=2),
+                in0=terms[:, :, 0, :],
+                in1=terms[:, :, 1, :],
+                op=ADD,
+            )
+            store(ng, 2 * half, res[:, 0, :])
+            store(ng, 2 * half + 1, res[:, 1, :])
 
         def copy_and_store(mt):
-            res = res_pool.tile([P, N_TILE], F32, name="res", tag="res")
-            nc.scalar.copy(out=res[:], in_=banks[(GROUPS - 1, mt)][:])
-            store(GROUPS - 1, mt, res)
+            res = result_tile(GROUPS - 1, mt)
+            nc.scalar.copy(
+                out=res[:, mt % 2, :], in_=banks[(GROUPS - 1, mt)][:].rearrange("p h c o -> p (h c o)")
+            )
+            store(GROUPS - 1, mt, res[:, mt % 2, :])
 
         all_tiles = list(range(TOKEN_TILES))
 
@@ -274,8 +296,7 @@ def tile_transformerblock_pa_kernel(tc, x, freqs_cos, freqs_sin, wq, wk, wv, out
             quantize_and_multiply(first)
             quantize_and_multiply(first + 1)
             interleave_up_to(first + 3 + LOOK)
-            for mt in range(GPSIMD_ADDS, TOKEN_TILES):
-                add_and_store(c, mt, nc.vector)
+            add_pair_and_store(c, 1)
             quantize_and_multiply(first + 2)
             quantize_and_multiply(first + 3)
 

@@ -27,9 +27,13 @@ HALF = 64
 FLOPS = 2 * TOKENS * K * (GROUPS * N_TILE)
 
 LOOK = 3
-SPLIT = 304
+SPLIT = 464
 HEAD_VECTOR_UNITS = (0, 1, 3, 5, 6)
 GPSIMD_ADDS = 2
+ACC_BANKS = 6
+STAGE_BANKS = 2
+PAIR_BUFS = 4
+TENSOR_UNITS = (10, 14, 18, 22)
 
 
 def scalar_columns(u):
@@ -50,12 +54,13 @@ def tile_transformerblock_pa_kernel(tc, x, freqs_cos, freqs_sin, wq, wk, wv, out
 
     with ExitStack() as ctx:
         const = ctx.enter_context(tc.tile_pool(name="const", bufs=1))
-        wg_pool = ctx.enter_context(tc.tile_pool(name="wg", bufs=7))
+        wg_pool = ctx.enter_context(tc.tile_pool(name="wg", bufs=PAIR_BUFS))
         xg_pool = ctx.enter_context(tc.tile_pool(name="xg", bufs=2))
         wc_pool = ctx.enter_context(tc.tile_pool(name="wc", bufs=3))
         res_pool = ctx.enter_context(tc.tile_pool(name="res", bufs=6))
         prod_pool = ctx.enter_context(tc.tile_pool(name="prod", bufs=2))
-        psum = ctx.enter_context(tc.psum_pool(name="psum", bufs=8))
+        psum = ctx.enter_context(tc.psum_pool(name="psum", bufs=ACC_BANKS))
+        stage_pool = ctx.enter_context(tc.psum_pool(name="stage", bufs=STAGE_BANKS))
         ctx.enter_context(tc.manual_schedule())
 
         cos_sb = const.tile([P, TOKEN_TILES, HALF, 1], BF16, name="cos_sb", tag="cos_sb")
@@ -107,18 +112,25 @@ def tile_transformerblock_pa_kernel(tc, x, freqs_cos, freqs_sin, wq, wk, wv, out
 
         ident = const.tile([P, P], F32, name="ident", tag="ident")
         make_identity(nc, ident[:])
+        ident_bf = const.tile([P, P], BF16, name="ident_bf", tag="ident_bf")
+        make_identity(nc, ident_bf[:])
+        warm = const.tile([P, 1], BF16, name="warm", tag="warm")
+        nc.scalar.copy(out=warm[:], in_=ident_bf[:, 0:1])
 
         table = const.tile([P, TOKEN_TILES, 2 * HALF, 2], BF16, name="table", tag="table")
-        by_pair = table[:].rearrange("p t (i a) b -> p t i (a b)", a=2)
-        nc.vector.tensor_copy(out=by_pair[:, :, :, 0:1], in_=cos_sb[:])
-        nc.vector.tensor_copy(out=by_pair[:, :, :, 1:2], in_=sin_sb[:])
-        nc.vector.tensor_scalar_mul(out=by_pair[:, :, :, 2:3], in0=sin_sb[:], scalar1=-1.0)
-        nc.vector.tensor_copy(out=by_pair[:, :, :, 3:4], in_=cos_sb[:])
+
+        def build_table():
+            by_pair = table[:].rearrange("p t (i a) b -> p t i (a b)", a=2)
+            nc.vector.tensor_copy(out=by_pair[:, :, :, 0:1], in_=cos_sb[:])
+            nc.vector.tensor_copy(out=by_pair[:, :, :, 1:2], in_=sin_sb[:])
+            nc.vector.tensor_scalar_mul(out=by_pair[:, :, :, 2:3], in0=sin_sb[:], scalar1=-1.0)
+            nc.vector.tensor_copy(out=by_pair[:, :, :, 3:4], in_=cos_sb[:])
 
         x_codes = const.tile([P, TOKEN_TILES, PASSES, P], U32, name="x_codes", tag="x_codes", align_bytes=64)
         x_scales = const.tile([P, TOKEN_TILES, PASSES, P], U8, name="x_scales", tag="x_scales", align_bytes=64)
 
-        grouped = {}
+        pairs = {}
+        staged = {}
         codes = {}
         banks = {}
         x_banks = {}
@@ -127,9 +139,32 @@ def tile_transformerblock_pa_kernel(tc, x, freqs_cos, freqs_sin, wq, wk, wv, out
         prods = {}
         issued = [0]
 
+        def stage(u):
+            if u not in TENSOR_UNITS:
+                return
+            for s in range(2):
+                st = stage_pool.tile([P, 2 * N_TILE], BF16, name="stage", tag="stage")
+                staged[(u, s)] = st
+                for q in range(2):
+                    c0 = (2 * s + q) * P
+                    nc.tensor.matmul(
+                        out=st[:, q * N_TILE : (q + 1) * N_TILE],
+                        lhsT=ident_bf[:],
+                        rhs=raw[u][:, :, c0 : c0 + P].rearrange("p j c -> p c j"),
+                        start=True,
+                        stop=True,
+                    )
+
         def interleave(u):
-            t = wg_pool.tile([P, N_TILE, PACK], BF16, name="wgrp", tag="wgrp", align_bytes=64)
-            grouped[u] = t
+            if u % 2 == 0:
+                pairs[u // 2] = wg_pool.tile([P, 2, N_TILE, PACK], BF16, name="wgrp", tag="wgrp", align_bytes=64)
+            t = pairs[u // 2][:, u % 2, :, :]
+            if u in TENSOR_UNITS:
+                for s in range(2):
+                    nc.scalar.copy(
+                        out=t[:, 2 * s * P : 2 * (s + 1) * P, :].rearrange("p c j -> p (c j)"), in_=staged[(u, s)][:]
+                    )
+                return
             cut = scalar_columns(u)
             if cut > 0:
                 nc.scalar.copy(out=t[:, 0:cut, :], in_=raw[u][:, :, 0:cut].rearrange("p j c -> p c j"))
@@ -143,7 +178,7 @@ def tile_transformerblock_pa_kernel(tc, x, freqs_cos, freqs_sin, wq, wk, wv, out
                 interleave(issued[0])
                 issued[0] += 1
 
-        def quantize(u):
+        def quantize(u, count=1):
             ng, g = divmod(u, PASSES)
             if g == 0:
                 wc = wc_pool.tile([P, PASSES, N_TILE], U32, name="wcodes", tag="wcodes", align_bytes=64)
@@ -151,9 +186,9 @@ def tile_transformerblock_pa_kernel(tc, x, freqs_cos, freqs_sin, wq, wk, wv, out
                 codes[ng] = (wc, ws)
             wc, ws = codes[ng]
             nc.vector.quantize_mx(
-                out=wc[:, g, :].bitcast(FP8X4),
-                scales=ws[:, g, :],
-                in_=grouped[u][:].rearrange("p c j -> p (c j)"),
+                out=wc[:, g : g + count, :].rearrange("p g c -> p (g c)").bitcast(FP8X4),
+                scales=ws[:, g : g + count, :].rearrange("p g c -> p (g c)"),
+                in_=pairs[u // 2][:, u % 2 : u % 2 + count, :, :].rearrange("p h c j -> p (h c j)"),
             )
 
         def multiply(u, token_tiles):
@@ -177,7 +212,10 @@ def tile_transformerblock_pa_kernel(tc, x, freqs_cos, freqs_sin, wq, wk, wv, out
         def transpose_x(mt):
             words = x_sb[mt][:].bitcast(F32)
             for half in range(2):
-                xt = psum.tile([P, 2, 2, P], F32, name="bank", tag="bank")
+                if mt < TOKEN_TILES - 1:
+                    xt = psum.tile([P, 2, 2, P], F32, name="bank", tag="bank")
+                else:
+                    xt = stage_pool.tile([P, 2, 2, P], F32, name="stage", tag="stage")
                 x_banks[(mt, half)] = xt
                 for gl in range(2):
                     g = 2 * half + gl
@@ -260,16 +298,17 @@ def tile_transformerblock_pa_kernel(tc, x, freqs_cos, freqs_sin, wq, wk, wv, out
             quantize(u)
             multiply(u, all_tiles)
 
+        early_tiles = [0, 1]
+
         interleave_up_to(2)
         for mt in all_tiles:
             transpose_x(mt)
-        quantize(0)
-        quantize(1)
+        quantize(0, 2)
         gather_x(0)
         interleave_up_to(4)
-        quantize(2)
-        quantize(3)
+        quantize(2, 2)
         quantize_x(0)
+        build_table()
         quantize(4)
         gather_x(1)
         interleave_up_to(5)
@@ -283,26 +322,36 @@ def tile_transformerblock_pa_kernel(tc, x, freqs_cos, freqs_sin, wq, wk, wv, out
         for mt in all_tiles:
             for g in range(PASSES):
                 multiply(g, [mt])
-        multiply(4, all_tiles)
-        multiply(5, all_tiles)
+        multiply(4, early_tiles)
+        multiply(5, early_tiles)
 
         for c in range(GROUPS - 2):
+            stage(PASSES * (c + 1) + 6)
             for mt in all_tiles:
                 rotate(c, mt)
+                if mt < 2:
+                    multiply(PASSES * (c + 1), [mt + 2])
+                    multiply(PASSES * (c + 1) + 1, [mt + 2])
                 if 0 < mt <= GPSIMD_ADDS:
                     add_and_store(c, mt - 1, nc.gpsimd)
             first = PASSES * (c + 1) + 2
             interleave_up_to(first + 1)
-            quantize_and_multiply(first)
-            quantize_and_multiply(first + 1)
+            quantize(first, 2)
+            multiply(first, all_tiles)
+            multiply(first + 1, all_tiles)
             interleave_up_to(first + 3 + LOOK)
             add_pair_and_store(c, 1)
-            quantize_and_multiply(first + 2)
-            quantize_and_multiply(first + 3)
+            quantize(first + 2, 2)
+            multiply(first + 2, early_tiles)
+            multiply(first + 3, early_tiles)
 
         last = GROUPS - 2
         rotate(last, 0)
+        multiply(UNITS - 4, [2])
+        multiply(UNITS - 3, [2])
         rotate(last, 1)
+        multiply(UNITS - 4, [3])
+        multiply(UNITS - 3, [3])
         add_and_store(last, 0, nc.gpsimd)
         quantize_and_multiply(UNITS - 2)
         add_and_store(last, 1, nc.vector)

@@ -104,7 +104,9 @@ def tile_transformerblock_pa_kernel(tc, x, freqs_cos, freqs_sin, wq, wk, wv, out
         load_w(wq, 2, N_TILE, N_TILE, 1)
         load_w(wq, 3, N_TILE, N_TILE, 1)
         for g in range(PASSES):
-            load_w(wq, g, 2 * N_TILE, 2 * N_TILE, 2)
+            load_w(wq, g, 2 * N_TILE, N_TILE, 2)
+        for g in range(PASSES):
+            load_w(wq, g, 3 * N_TILE, N_TILE, 3)
         for g in range(PASSES):
             load_w(wk, g, 0, N_TILE, 4)
         for g in range(PASSES):

@@ -34,6 +34,7 @@ ACC_BANKS = 6
 STAGE_BANKS = 2
 PAIR_BUFS = 4
 TENSOR_UNITS = (10, 14, 18, 22)
+LOAD_ORDER = (0, 1, 2, -1, 3, 4, -2, -3, 5, -4, 6, 7)
 
 
 def scalar_columns(u):
@@ -50,7 +51,8 @@ def tile_transformerblock_pa_kernel(tc, x, freqs_cos, freqs_sin, wq, wk, wv, out
     q_out = out_0.rearrange("b s h d -> (b s) (h d)")
     k_out = out_1.rearrange("b s h d -> (b s) (h d)")
     v_out = out_2.rearrange("b s h d -> (b s) (h d)")
-    o_of = [(q_out, 0), (q_out, 512), (q_out, 1024), (q_out, 1536), (k_out, 0), (v_out, 0)]
+    o_of = [(k_out, 0), (q_out, 0), (q_out, 512), (q_out, 1024), (q_out, 1536), (v_out, 0)]
+    w_of = [(wk, 0), (wq, 0), (wq, 512), (wq, 1024), (wq, 1536), (wv, 0)]
 
     with ExitStack() as ctx:
         const = ctx.enter_context(tc.tile_pool(name="const", bufs=1))
@@ -91,26 +93,17 @@ def tile_transformerblock_pa_kernel(tc, x, freqs_cos, freqs_sin, wq, wk, wv, out
             nc.sync.dma_start(out=t[:], in_=x_rows[mt * P : (mt + 1) * P, :])
             x_sb[mt] = t
 
-        load_w(wq, 0, 0, N_TILE, 0)
-        load_w(wq, 1, 0, N_TILE, 0)
-        load_w(wq, 2, 0, N_TILE, 0)
-        load_x(0)
-        load_w(wq, 3, 0, N_TILE, 0)
-        load_w(wq, 0, N_TILE, N_TILE, 1)
-        load_x(1)
-        load_x(2)
-        load_w(wq, 1, N_TILE, N_TILE, 1)
-        load_x(3)
-        load_w(wq, 2, N_TILE, N_TILE, 1)
-        load_w(wq, 3, N_TILE, N_TILE, 1)
-        for g in range(PASSES):
-            load_w(wq, g, 2 * N_TILE, N_TILE, 2)
-        for g in range(PASSES):
-            load_w(wq, g, 3 * N_TILE, N_TILE, 3)
-        for g in range(PASSES):
-            load_w(wk, g, 0, N_TILE, 4)
-        for g in range(PASSES):
-            load_w(wv, g, 0, N_TILE, 5)
+        def load_unit(u):
+            w, c0 = w_of[u // PASSES]
+            load_w(w, u % PASSES, c0, N_TILE, u // PASSES)
+
+        for step in LOAD_ORDER:
+            if step < 0:
+                load_x(-step - 1)
+            else:
+                load_unit(step)
+        for u in range(8, UNITS):
+            load_unit(u)
 
         ident = const.tile([P, P], F32, name="ident", tag="ident")
         make_identity(nc, ident[:])

@@ -65,16 +65,9 @@ def tile_transformerblock_pa_kernel(tc, x, freqs_cos, freqs_sin, wq, wk, wv, out
         stage_pool = ctx.enter_context(tc.psum_pool(name="stage", bufs=STAGE_BANKS))
         ctx.enter_context(tc.manual_schedule())
 
-        cos_sb = const.tile([P, TOKEN_TILES, HALF, 1], BF16, name="cos_sb", tag="cos_sb")
-        sin_sb = const.tile([P, TOKEN_TILES, HALF, 1], BF16, name="sin_sb", tag="sin_sb")
-        nc.scalar.dma_start(
-            out=sin_sb[:].rearrange("p t i o -> p t (i o)"),
-            in_=freqs_sin.rearrange("(t p) i -> p t i", p=P),
-        )
-        nc.scalar.dma_start(
-            out=cos_sb[:].rearrange("p t i o -> p t (i o)"),
-            in_=freqs_cos.rearrange("(t p) i -> p t i", p=P),
-        )
+        factors = const.tile([P, 4, TOKEN_TILES, HALF], BF16, name="factors", tag="factors")
+        nc.scalar.dma_start(out=factors[:, 1, :, :], in_=freqs_sin.rearrange("(t p) i -> p t i", p=P))
+        nc.scalar.dma_start(out=factors[:, 0, :, :], in_=freqs_cos.rearrange("(t p) i -> p t i", p=P))
 
         raw = {}
         x_sb = {}
@@ -113,13 +106,11 @@ def tile_transformerblock_pa_kernel(tc, x, freqs_cos, freqs_sin, wq, wk, wv, out
         nc.scalar.copy(out=warm[:], in_=ident_bf[:, 0:1])
 
         table = const.tile([P, TOKEN_TILES, 2 * HALF, 2], BF16, name="table", tag="table")
-
-        def build_table():
-            by_pair = table[:].rearrange("p t (i a) b -> p t i (a b)", a=2)
-            nc.vector.tensor_copy(out=by_pair[:, :, :, 0:1], in_=cos_sb[:])
-            nc.vector.tensor_copy(out=by_pair[:, :, :, 1:2], in_=sin_sb[:])
-            nc.vector.tensor_scalar_mul(out=by_pair[:, :, :, 2:3], in0=sin_sb[:], scalar1=-1.0)
-            nc.vector.tensor_copy(out=by_pair[:, :, :, 3:4], in_=cos_sb[:])
+        nc.scalar.mul(out=factors[:, 2, :, :], in_=factors[:, 1, :, :], mul=-1.0)
+        nc.scalar.copy(out=factors[:, 3, :, :], in_=factors[:, 0, :, :])
+        nc.scalar.copy(
+            out=table[:].rearrange("p t (i a) b -> p t i (a b)", a=2), in_=factors[:].rearrange("p k t i -> p t i k")
+        )
 
         x_codes = const.tile([P, TOKEN_TILES, PASSES, P], U32, name="x_codes", tag="x_codes", align_bytes=64)
         x_scales = const.tile([P, TOKEN_TILES, PASSES, P], U8, name="x_scales", tag="x_scales", align_bytes=64)
@@ -303,7 +294,6 @@ def tile_transformerblock_pa_kernel(tc, x, freqs_cos, freqs_sin, wq, wk, wv, out
         interleave_up_to(4)
         quantize(2, 2)
         quantize_x(0)
-        build_table()
         quantize(4)
         gather_x(1)
         interleave_up_to(5)

@@ -30,8 +30,8 @@ LOOK = 3
 SPLIT = 464
 HEAD_VECTOR_UNITS = (0, 1, 3, 5, 6)
 GPSIMD_ADDS = 2
-ACC_BANKS = 6
-STAGE_BANKS = 2
+ACC_BANKS = 4
+STAGE_BANKS = 4
 PAIR_BUFS = 4
 TENSOR_UNITS = (10, 14, 18, 22)
 LOAD_ORDER = (0, 1, 2, -1, 3, 4, -2, -3, 5, -4, 6, 7)
@@ -182,7 +182,10 @@ def tile_transformerblock_pa_kernel(tc, x, freqs_cos, freqs_sin, wq, wk, wv, out
             wc, ws = codes[ng]
             for mt in token_tiles:
                 if g == 0:
-                    acc = psum.tile([P, HEADS_PER_GROUP, 2 * HALF, 1], F32, name="bank", tag="bank")
+                    if ng == GROUPS - 1:
+                        acc = stage_pool.tile([P, HEADS_PER_GROUP, 2 * HALF, 1], F32, name="stage", tag="stage")
+                    else:
+                        acc = psum.tile([P, HEADS_PER_GROUP, 2 * HALF, 1], F32, name="bank", tag="bank")
                     banks[(ng, mt)] = acc
                 acc = banks[(ng, mt)]
                 nc.tensor.matmul_mx(
@@ -198,7 +201,7 @@ def tile_transformerblock_pa_kernel(tc, x, freqs_cos, freqs_sin, wq, wk, wv, out
         def transpose_x(mt):
             words = x_sb[mt][:].bitcast(F32)
             for half in range(2):
-                if mt < TOKEN_TILES - 1:
+                if mt < 2:
                     xt = psum.tile([P, 2, 2, P], F32, name="bank", tag="bank")
                 else:
                     xt = stage_pool.tile([P, 2, 2, P], F32, name="stage", tag="stage")
@@ -284,8 +287,6 @@ def tile_transformerblock_pa_kernel(tc, x, freqs_cos, freqs_sin, wq, wk, wv, out
             quantize(u)
             multiply(u, all_tiles)
 
-        early_tiles = [0, 1]
-
         interleave_up_to(2)
         for mt in all_tiles:
             transpose_x(mt)
@@ -307,36 +308,31 @@ def tile_transformerblock_pa_kernel(tc, x, freqs_cos, freqs_sin, wq, wk, wv, out
         for mt in all_tiles:
             for g in range(PASSES):
                 multiply(g, [mt])
-        multiply(4, early_tiles)
-        multiply(5, early_tiles)
 
         for c in range(GROUPS - 2):
-            stage(PASSES * (c + 1) + 6)
+            first = PASSES * (c + 1) + 2
+            stage(first + 4)
             for mt in all_tiles:
                 rotate(c, mt)
-                if mt < 2:
-                    multiply(PASSES * (c + 1), [mt + 2])
-                    multiply(PASSES * (c + 1) + 1, [mt + 2])
+                multiply(first - 2, [mt])
+                multiply(first - 1, [mt])
                 if 0 < mt <= GPSIMD_ADDS:
                     add_and_store(c, mt - 1, nc.gpsimd)
-            first = PASSES * (c + 1) + 2
             interleave_up_to(first + 1)
             quantize(first, 2)
-            multiply(first, all_tiles)
-            multiply(first + 1, all_tiles)
+            for mt in all_tiles:
+                multiply(first, [mt])
+                multiply(first + 1, [mt])
+            stage(first + 6)
             interleave_up_to(first + 3 + LOOK)
             add_pair_and_store(c, 1)
             quantize(first + 2, 2)
-            multiply(first + 2, early_tiles)
-            multiply(first + 3, early_tiles)
 
         last = GROUPS - 2
+        multiply(UNITS - 4, all_tiles)
+        multiply(UNITS - 3, all_tiles)
         rotate(last, 0)
-        multiply(UNITS - 4, [2])
-        multiply(UNITS - 3, [2])
         rotate(last, 1)
-        multiply(UNITS - 4, [3])
-        multiply(UNITS - 3, [3])
         add_and_store(last, 0, nc.gpsimd)
         quantize_and_multiply(UNITS - 2)
         add_and_store(last, 1, nc.vector)

@@ -28,6 +28,7 @@ FLOPS = 2 * TOKENS * K * (GROUPS * N_TILE)
 
 LOOK = 3
 SPLIT = 464
+RUN = 8
 HEAD_VECTOR_UNITS = (0, 1, 3, 5, 6)
 GPSIMD_ADDS = 2
 ACC_BANKS = 4
@@ -153,10 +154,14 @@ def tile_transformerblock_pa_kernel(tc, x, freqs_cos, freqs_sin, wq, wk, wv, out
                 return
             cut = scalar_columns(u)
             if cut > 0:
-                nc.scalar.copy(out=t[:, 0:cut, :], in_=raw[u][:, :, 0:cut].rearrange("p j c -> p c j"))
+                nc.scalar.copy(
+                    out=t[:, 0:cut, :].rearrange("p (b i) j -> p b j i", i=RUN),
+                    in_=raw[u][:, :, 0:cut].rearrange("p j (b i) -> p b j i", i=RUN),
+                )
             if cut < N_TILE:
                 nc.vector.tensor_copy(
-                    out=t[:, cut:N_TILE, :], in_=raw[u][:, :, cut:N_TILE].rearrange("p j c -> p c j")
+                    out=t[:, cut:N_TILE, :].rearrange("p (b i) j -> p b j i", i=RUN),
+                    in_=raw[u][:, :, cut:N_TILE].rearrange("p j (b i) -> p b j i", i=RUN),
                 )
 
         def interleave_up_to(u):

@@ -48,10 +48,10 @@ def scalar_columns(u):
 
 def tile_transformerblock_pa_kernel(tc, x, freqs_cos, freqs_sin, wq, wk, wv, out_0, out_1, out_2):
     nc = tc.nc
-    x_rows = x.flatten_outer_dims()
-    q_out = out_0.rearrange("b s h d -> (b s) (h d)")
-    k_out = out_1.rearrange("b s h d -> (b s) (h d)")
-    v_out = out_2.rearrange("b s h d -> (b s) (h d)")
+    x_rows = x.flatten_outer_dims().rearrange("(p t) k -> t p k", t=TOKEN_TILES)
+    q_out = out_0.rearrange("b (p t) h d -> t (b p) (h d)", t=TOKEN_TILES)
+    k_out = out_1.rearrange("b (p t) h d -> t (b p) (h d)", t=TOKEN_TILES)
+    v_out = out_2.rearrange("b (p t) h d -> t (b p) (h d)", t=TOKEN_TILES)
     o_of = [(k_out, 0), (q_out, 0), (q_out, 512), (q_out, 1024), (q_out, 1536), (v_out, 0)]
     w_of = [(wk, 0), (wq, 0), (wq, 512), (wq, 1024), (wq, 1536), (wv, 0)]
 
@@ -67,8 +67,8 @@ def tile_transformerblock_pa_kernel(tc, x, freqs_cos, freqs_sin, wq, wk, wv, out
         ctx.enter_context(tc.manual_schedule())
 
         factors = const.tile([P, 4, TOKEN_TILES, HALF], BF16, name="factors", tag="factors")
-        nc.scalar.dma_start(out=factors[:, 1, :, :], in_=freqs_sin.rearrange("(t p) i -> p t i", p=P))
-        nc.scalar.dma_start(out=factors[:, 0, :, :], in_=freqs_cos.rearrange("(t p) i -> p t i", p=P))
+        nc.scalar.dma_start(out=factors[:, 1, :, :], in_=freqs_sin.rearrange("(p t) i -> p t i", t=TOKEN_TILES))
+        nc.scalar.dma_start(out=factors[:, 0, :, :], in_=freqs_cos.rearrange("(p t) i -> p t i", t=TOKEN_TILES))
 
         raw = {}
         x_sb = {}
@@ -84,7 +84,7 @@ def tile_transformerblock_pa_kernel(tc, x, freqs_cos, freqs_sin, wq, wk, wv, out
 
         def load_x(mt):
             t = const.tile([P, K], BF16, name="x_sb%d" % mt, tag="x_sb%d" % mt)
-            nc.sync.dma_start(out=t[:], in_=x_rows[mt * P : (mt + 1) * P, :])
+            nc.sync.dma_start(out=t[:], in_=x_rows[mt, :, :])
             x_sb[mt] = t
 
         def load_unit(u):
@@ -236,7 +236,7 @@ def tile_transformerblock_pa_kernel(tc, x, freqs_cos, freqs_sin, wq, wk, wv, out
 
         def store(ng, mt, res):
             o_ap, c0 = o_of[ng]
-            nc.sync.dma_start(out=o_ap[mt * P : (mt + 1) * P, c0 : c0 + N_TILE], in_=res)
+            nc.sync.dma_start(out=o_ap[mt, :, c0 : c0 + N_TILE], in_=res)
 
         def rotate(ng, mt):
             if mt % 2 == 0:

@@ -336,12 +336,12 @@ def tile_transformerblock_pa_kernel(tc, x, freqs_cos, freqs_sin, wq, wk, wv, out
         last = GROUPS - 2
         multiply(UNITS - 4, all_tiles)
         multiply(UNITS - 3, all_tiles)
-        rotate(last, 0)
-        rotate(last, 1)
-        add_and_store(last, 0, nc.gpsimd)
         quantize_and_multiply(UNITS - 2)
-        add_and_store(last, 1, nc.vector)
+        rotate(last, 0)
+        add_and_store(last, 0, nc.gpsimd)
         quantize_and_multiply(UNITS - 1)
+        rotate(last, 1)
+        add_and_store(last, 1, nc.vector)
         for mt in all_tiles:
             copy_and_store(mt)
         rotate(last, 2)

@@ -27,10 +27,9 @@ HALF = 64
 FLOPS = 2 * TOKENS * K * (GROUPS * N_TILE)
 
 LOOK = 3
-SPLIT = 464
+SPLIT = 384
 RUN = 8
-HEAD_VECTOR_UNITS = (0, 1, 3, 5, 6)
-GPSIMD_ADDS = 2
+HEAD_VECTOR_UNITS = (0, 1, 3, 5)
 ACC_BANKS = 4
 STAGE_BANKS = 4
 PAIR_BUFS = 4
@@ -41,6 +40,8 @@ LOAD_ORDER = (0, 1, 2, -1, 3, 4, -2, -3, 5, -4, 6, 7)
 def scalar_columns(u):
     if u in HEAD_VECTOR_UNITS:
         return 0
+    if u == 6:
+        return 256
     if u >= 7 and u % PASSES == PASSES - 1:
         return SPLIT
     return N_TILE
@@ -57,11 +58,12 @@ def tile_transformerblock_pa_kernel(tc, x, freqs_cos, freqs_sin, wq, wk, wv, out
 
     with ExitStack() as ctx:
         const = ctx.enter_context(tc.tile_pool(name="const", bufs=1))
+        raw_pool = ctx.enter_context(tc.tile_pool(name="raw", bufs=24))
         wg_pool = ctx.enter_context(tc.tile_pool(name="wg", bufs=PAIR_BUFS))
         xg_pool = ctx.enter_context(tc.tile_pool(name="xg", bufs=2))
         wc_pool = ctx.enter_context(tc.tile_pool(name="wc", bufs=3))
         res_pool = ctx.enter_context(tc.tile_pool(name="res", bufs=6))
-        prod_pool = ctx.enter_context(tc.tile_pool(name="prod", bufs=2))
+        prod_pool = ctx.enter_context(tc.tile_pool(name="prod", bufs=3))
         psum = ctx.enter_context(tc.psum_pool(name="psum", bufs=ACC_BANKS))
         stage_pool = ctx.enter_context(tc.psum_pool(name="stage", bufs=STAGE_BANKS))
         ctx.enter_context(tc.manual_schedule())
@@ -74,7 +76,7 @@ def tile_transformerblock_pa_kernel(tc, x, freqs_cos, freqs_sin, wq, wk, wv, out
         x_sb = {}
 
         def load_w(w, g, c0, width, first_group):
-            t = const.tile([P, PACK, width], BF16, name="raw%d_%d" % (first_group, g), tag="raw%d_%d" % (first_group, g))
+            t = raw_pool.tile([P, PACK, width], BF16, name="raw", tag="raw")
             nc.sync.dma_start(
                 out=t[:],
                 in_=w[g * K_PASS : (g + 1) * K_PASS, c0 : c0 + width].rearrange("(p j) c -> p j c", j=PACK),
@@ -83,7 +85,7 @@ def tile_transformerblock_pa_kernel(tc, x, freqs_cos, freqs_sin, wq, wk, wv, out
                 raw[(first_group + n) * PASSES + g] = t[:, :, n * N_TILE : (n + 1) * N_TILE]
 
         def load_x(mt):
-            t = const.tile([P, K], BF16, name="x_sb%d" % mt, tag="x_sb%d" % mt)
+            t = raw_pool.tile([P, K], BF16, name="raw", tag="raw")
             nc.sync.dma_start(out=t[:], in_=x_rows[mt, :, :])
             x_sb[mt] = t
 
@@ -96,7 +98,7 @@ def tile_transformerblock_pa_kernel(tc, x, freqs_cos, freqs_sin, wq, wk, wv, out
                 load_x(-step - 1)
             else:
                 load_unit(step)
-        for u in range(8, UNITS):
+        for u in range(8, 20):
             load_unit(u)
 
         ident = const.tile([P, P], F32, name="ident", tag="ident")
@@ -115,6 +117,8 @@ def tile_transformerblock_pa_kernel(tc, x, freqs_cos, freqs_sin, wq, wk, wv, out
 
         x_codes = const.tile([P, TOKEN_TILES, PASSES, P], U32, name="x_codes", tag="x_codes", align_bytes=64)
         x_scales = const.tile([P, TOKEN_TILES, PASSES, P], U8, name="x_scales", tag="x_scales", align_bytes=64)
+
+        gate = const.tile([P, 8], U32, name="gate", tag="gate")
 
         pairs = {}
         staged = {}
@@ -252,7 +256,7 @@ def tile_transformerblock_pa_kernel(tc, x, freqs_cos, freqs_sin, wq, wk, wv, out
             )
 
         def result_tile(ng, mt):
-            if mt % 2 == 0:
+            if (ng, mt // 2) not in sums:
                 sums[(ng, mt // 2)] = res_pool.tile([P, 2, N_TILE], F32, name="res", tag="res")
             return sums[(ng, mt // 2)]
 
@@ -267,10 +271,13 @@ def tile_transformerblock_pa_kernel(tc, x, freqs_cos, freqs_sin, wq, wk, wv, out
             )
             store(ng, mt, res[:, mt % 2, :])
 
-        def add_pair_and_store(ng, half):
+        def wait_for_codes(u):
+            nc.gpsimd.tensor_copy(out=gate[:], in_=codes[u // PASSES][0][:, u % PASSES, 0:8])
+
+        def add_pair_and_store(ng, half, engine):
             res = result_tile(ng, 2 * half)
             terms = prods[(ng, half)][:].rearrange("p t h (i a) b -> p (t h i) a b", a=2)
-            nc.vector.tensor_tensor(
+            engine.tensor_tensor(
                 out=res[:].rearrange("p t (n b) -> p (t n) b", b=2),
                 in0=terms[:, :, 0, :],
                 in1=terms[:, :, 1, :],
@@ -306,23 +313,30 @@ def tile_transformerblock_pa_kernel(tc, x, freqs_cos, freqs_sin, wq, wk, wv, out
         quantize_x(1)
         gather_x(2)
         quantize_x(2)
-        interleave_up_to(6)
         gather_x(3)
+        interleave_up_to(6)
         quantize_x(3)
         quantize(5)
         for mt in all_tiles:
             for g in range(PASSES):
                 multiply(g, [mt])
 
+        for u in range(20, UNITS):
+            load_unit(u)
+
         for c in range(GROUPS - 2):
             first = PASSES * (c + 1) + 2
-            stage(first + 4)
+            if c > 0:
+                stage(first + 4)
+                wait_for_codes(first - 1)
+                add_pair_and_store(c - 1, 1, nc.gpsimd)
             for mt in all_tiles:
+                if c == 0 and mt == 2:
+                    stage(first + 4)
                 rotate(c, mt)
                 multiply(first - 2, [mt])
                 multiply(first - 1, [mt])
-                if 0 < mt <= GPSIMD_ADDS:
-                    add_and_store(c, mt - 1, nc.gpsimd)
+            add_and_store(c, 0, nc.gpsimd)
             interleave_up_to(first + 1)
             quantize(first, 2)
             for mt in all_tiles:
@@ -330,21 +344,23 @@ def tile_transformerblock_pa_kernel(tc, x, freqs_cos, freqs_sin, wq, wk, wv, out
                 multiply(first + 1, [mt])
             stage(first + 6)
             interleave_up_to(first + 3 + LOOK)
-            add_pair_and_store(c, 1)
+            add_and_store(c, 1, nc.vector)
             quantize(first + 2, 2)
 
         last = GROUPS - 2
         multiply(UNITS - 4, all_tiles)
         multiply(UNITS - 3, all_tiles)
         quantize_and_multiply(UNITS - 2)
+        wait_for_codes(UNITS - 2)
+        add_pair_and_store(last - 1, 1, nc.gpsimd)
         rotate(last, 0)
-        add_and_store(last, 0, nc.gpsimd)
-        quantize_and_multiply(UNITS - 1)
         rotate(last, 1)
+        add_and_store(last, 0, nc.vector)
+        quantize_and_multiply(UNITS - 1)
         add_and_store(last, 1, nc.vector)
+        rotate(last, 2)
         for mt in all_tiles:
             copy_and_store(mt)
-        rotate(last, 2)
+        add_and_store(last, 2, nc.gpsimd)
         rotate(last, 3)
-        add_and_store(last, 2, nc.vector)
         add_and_store(last, 3, nc.vector)

@@ -27,7 +27,7 @@ HALF = 64
 FLOPS = 2 * TOKENS * K * (GROUPS * N_TILE)
 
 LOOK = 3
-SPLIT = 384
+SPLIT = 448
 RUN = 8
 HEAD_VECTOR_UNITS = (0, 1, 3, 5)
 ACC_BANKS = 4

@@ -27,24 +27,17 @@ HALF = 64
 FLOPS = 2 * TOKENS * K * (GROUPS * N_TILE)
 
 LOOK = 3
-SPLIT = 448
 RUN = 8
-HEAD_VECTOR_UNITS = (0, 1, 3, 5)
+SCALAR_COLUMNS = {0: 0, 1: 0, 3: 0, 5: 0, 6: 256, 7: 384, 11: 256}
 ACC_BANKS = 4
 STAGE_BANKS = 4
 PAIR_BUFS = 4
-TENSOR_UNITS = (10, 14, 18, 22)
+TENSOR_UNITS = (14, 18, 22)
 LOAD_ORDER = (0, 1, 2, -1, 3, 4, -2, -3, 5, -4, 6, 7)
 
 
 def scalar_columns(u):
-    if u in HEAD_VECTOR_UNITS:
-        return 0
-    if u == 6:
-        return 256
-    if u >= 7 and u % PASSES == PASSES - 1:
-        return SPLIT
-    return N_TILE
+    return SCALAR_COLUMNS.get(u, N_TILE)
 
 
 def tile_transformerblock_pa_kernel(tc, x, freqs_cos, freqs_sin, wq, wk, wv, out_0, out_1, out_2):
@@ -331,8 +324,6 @@ def tile_transformerblock_pa_kernel(tc, x, freqs_cos, freqs_sin, wq, wk, wv, out
                 wait_for_codes(first - 1)
                 add_pair_and_store(c - 1, 1, nc.gpsimd)
             for mt in all_tiles:
-                if c == 0 and mt == 2:
-                    stage(first + 4)
                 rotate(c, mt)
                 multiply(first - 2, [mt])
                 multiply(first - 1, [mt])

from contextlib import ExitStack

import concourse.mybir as mybir
from concourse.masks import make_identity

F32 = mybir.dt.float32
BF16 = mybir.dt.bfloat16
U32 = mybir.dt.uint32
U8 = mybir.dt.uint8
FP8X4 = mybir.dt.float8_e5m2_x4
MULT = mybir.AluOpType.mult
ADD = mybir.AluOpType.add

P = 128
PACK = 4
K = 2048
K_PASS = P * PACK
PASSES = K // K_PASS
TOKENS = 512
TOKEN_TILES = TOKENS // P
N_TILE = 512
GROUPS = 6
UNITS = GROUPS * PASSES
HEADS_PER_GROUP = 4
HALF = 64

FLOPS = 2 * TOKENS * K * (GROUPS * N_TILE)

LOOK = 3
RUN = 8
SCALAR_COLUMNS = {0: 0, 1: 0, 3: 0, 5: 0, 6: 256, 7: 384, 11: 256}
ACC_BANKS = 4
STAGE_BANKS = 4
PAIR_BUFS = 4
TENSOR_UNITS = (14, 18, 22)
LOAD_ORDER = (0, 1, 2, -1, 3, 4, -2, -3, 5, -4, 6, 7)


def scalar_columns(u):
    return SCALAR_COLUMNS.get(u, N_TILE)


def tile_transformerblock_pa_kernel(tc, x, freqs_cos, freqs_sin, wq, wk, wv, out_0, out_1, out_2):
    nc = tc.nc
    x_rows = x.flatten_outer_dims().rearrange("(p t) k -> t p k", t=TOKEN_TILES)
    q_out = out_0.rearrange("b (p t) h d -> t (b p) (h d)", t=TOKEN_TILES)
    k_out = out_1.rearrange("b (p t) h d -> t (b p) (h d)", t=TOKEN_TILES)
    v_out = out_2.rearrange("b (p t) h d -> t (b p) (h d)", t=TOKEN_TILES)
    o_of = [(k_out, 0), (q_out, 0), (q_out, 512), (q_out, 1024), (q_out, 1536), (v_out, 0)]
    w_of = [(wk, 0), (wq, 0), (wq, 512), (wq, 1024), (wq, 1536), (wv, 0)]

    with ExitStack() as ctx:
        const = ctx.enter_context(tc.tile_pool(name="const", bufs=1))
        raw_pool = ctx.enter_context(tc.tile_pool(name="raw", bufs=24))
        wg_pool = ctx.enter_context(tc.tile_pool(name="wg", bufs=PAIR_BUFS))
        xg_pool = ctx.enter_context(tc.tile_pool(name="xg", bufs=2))
        wc_pool = ctx.enter_context(tc.tile_pool(name="wc", bufs=3))
        res_pool = ctx.enter_context(tc.tile_pool(name="res", bufs=6))
        prod_pool = ctx.enter_context(tc.tile_pool(name="prod", bufs=3))
        psum = ctx.enter_context(tc.psum_pool(name="psum", bufs=ACC_BANKS))
        stage_pool = ctx.enter_context(tc.psum_pool(name="stage", bufs=STAGE_BANKS))
        ctx.enter_context(tc.manual_schedule())

        factors = const.tile([P, 4, TOKEN_TILES, HALF], BF16, name="factors", tag="factors")
        nc.scalar.dma_start(out=factors[:, 1, :, :], in_=freqs_sin.rearrange("(p t) i -> p t i", t=TOKEN_TILES))
        nc.scalar.dma_start(out=factors[:, 0, :, :], in_=freqs_cos.rearrange("(p t) i -> p t i", t=TOKEN_TILES))

        raw = {}
        x_sb = {}

        def load_w(w, g, c0, width, first_group):
            t = raw_pool.tile([P, PACK, width], BF16, name="raw", tag="raw")
            nc.sync.dma_start(
                out=t[:],
                in_=w[g * K_PASS : (g + 1) * K_PASS, c0 : c0 + width].rearrange("(p j) c -> p j c", j=PACK),
            )
            for n in range(width // N_TILE):
                raw[(first_group + n) * PASSES + g] = t[:, :, n * N_TILE : (n + 1) * N_TILE]

        def load_x(mt):
            t = raw_pool.tile([P, K], BF16, name="raw", tag="raw")
            nc.sync.dma_start(out=t[:], in_=x_rows[mt, :, :])
            x_sb[mt] = t

        def load_unit(u):
            w, c0 = w_of[u // PASSES]
            load_w(w, u % PASSES, c0, N_TILE, u // PASSES)

        for step in LOAD_ORDER:
            if step < 0:
                load_x(-step - 1)
            else:
                load_unit(step)
        for u in range(8, 20):
            load_unit(u)

        ident = const.tile([P, P], F32, name="ident", tag="ident")
        make_identity(nc, ident[:])
        ident_bf = const.tile([P, P], BF16, name="ident_bf", tag="ident_bf")
        make_identity(nc, ident_bf[:])
        warm = const.tile([P, 1], BF16, name="warm", tag="warm")
        nc.scalar.copy(out=warm[:], in_=ident_bf[:, 0:1])

        table = const.tile([P, TOKEN_TILES, 2 * HALF, 2], BF16, name="table", tag="table")
        nc.scalar.mul(out=factors[:, 2, :, :], in_=factors[:, 1, :, :], mul=-1.0)
        nc.scalar.copy(out=factors[:, 3, :, :], in_=factors[:, 0, :, :])
        nc.scalar.copy(
            out=table[:].rearrange("p t (i a) b -> p t i (a b)", a=2), in_=factors[:].rearrange("p k t i -> p t i k")
        )

        x_codes = const.tile([P, TOKEN_TILES, PASSES, P], U32, name="x_codes", tag="x_codes", align_bytes=64)
        x_scales = const.tile([P, TOKEN_TILES, PASSES, P], U8, name="x_scales", tag="x_scales", align_bytes=64)

        gate = const.tile([P, 8], U32, name="gate", tag="gate")

        pairs = {}
        staged = {}
        codes = {}
        banks = {}
        x_banks = {}
        x_grouped = {}
        sums = {}
        prods = {}
        issued = [0]

        def stage(u):
            if u not in TENSOR_UNITS:
                return
            for s in range(2):
                st = stage_pool.tile([P, 2 * N_TILE], BF16, name="stage", tag="stage")
                staged[(u, s)] = st
                for q in range(2):
                    c0 = (2 * s + q) * P
                    nc.tensor.matmul(
                        out=st[:, q * N_TILE : (q + 1) * N_TILE],
                        lhsT=ident_bf[:],
                        rhs=raw[u][:, :, c0 : c0 + P].rearrange("p j c -> p c j"),
                        start=True,
                        stop=True,
                    )

        def interleave(u):
            if u % 2 == 0:
                pairs[u // 2] = wg_pool.tile([P, 2, N_TILE, PACK], BF16, name="wgrp", tag="wgrp", align_bytes=64)
            t = pairs[u // 2][:, u % 2, :, :]
            if u in TENSOR_UNITS:
                for s in range(2):
                    nc.scalar.copy(
                        out=t[:, 2 * s * P : 2 * (s + 1) * P, :].rearrange("p c j -> p (c j)"), in_=staged[(u, s)][:]
                    )
                return
            cut = scalar_columns(u)
            if cut > 0:
                nc.scalar.copy(
                    out=t[:, 0:cut, :].rearrange("p (b i) j -> p b j i", i=RUN),
                    in_=raw[u][:, :, 0:cut].rearrange("p j (b i) -> p b j i", i=RUN),
                )
            if cut < N_TILE:
                nc.vector.tensor_copy(
                    out=t[:, cut:N_TILE, :].rearrange("p (b i) j -> p b j i", i=RUN),
                    in_=raw[u][:, :, cut:N_TILE].rearrange("p j (b i) -> p b j i", i=RUN),
                )

        def interleave_up_to(u):
            while issued[0] <= min(u, UNITS - 1):
                interleave(issued[0])
                issued[0] += 1

        def quantize(u, count=1):
            ng, g = divmod(u, PASSES)
            if g == 0:
                wc = wc_pool.tile([P, PASSES, N_TILE], U32, name="wcodes", tag="wcodes", align_bytes=64)
                ws = wc_pool.tile([P, PASSES, N_TILE], U8, name="wscales", tag="wscales", align_bytes=64)
                codes[ng] = (wc, ws)
            wc, ws = codes[ng]
            nc.vector.quantize_mx(
                out=wc[:, g : g + count, :].rearrange("p g c -> p (g c)").bitcast(FP8X4),
                scales=ws[:, g : g + count, :].rearrange("p g c -> p (g c)"),
                in_=pairs[u // 2][:, u % 2 : u % 2 + count, :, :].rearrange("p h c j -> p (h c j)"),
            )

        def multiply(u, token_tiles):
            ng, g = divmod(u, PASSES)
            wc, ws = codes[ng]
            for mt in token_tiles:
                if g == 0:
                    if ng == GROUPS - 1:
                        acc = stage_pool.tile([P, HEADS_PER_GROUP, 2 * HALF, 1], F32, name="stage", tag="stage")
                    else:
                        acc = psum.tile([P, HEADS_PER_GROUP, 2 * HALF, 1], F32, name="bank", tag="bank")
                    banks[(ng, mt)] = acc
                acc = banks[(ng, mt)]
                nc.tensor.matmul_mx(
                    out=acc[:].rearrange("p h c o -> p (h c o)"),
                    lhsT=x_codes[:, mt, g, :].bitcast(FP8X4),
                    lhsT_scale=x_scales[:, mt, g, :],
                    rhs=wc[:, g, :].bitcast(FP8X4),
                    rhs_scale=ws[:, g, :],
                    start=(g == 0),
                    stop=(g == PASSES - 1),
                )

        def transpose_x(mt):
            words = x_sb[mt][:].bitcast(F32)
            for half in range(2):
                if mt < 2:
                    xt = psum.tile([P, 2, 2, P], F32, name="bank", tag="bank")
                else:
                    xt = stage_pool.tile([P, 2, 2, P], F32, name="stage", tag="stage")
                x_banks[(mt, half)] = xt
                for gl in range(2):
                    g = 2 * half + gl
                    for s in range(2):
                        nc.tensor.transpose(
                            xt[:, gl, s, :], words[:, 256 * g + s : 256 * (g + 1) : 2], ident[:]
                        )

        def gather_x(mt):
            xg = xg_pool.tile([P, PASSES, P, PACK], BF16, name="xgrp", tag="xgrp", align_bytes=64)
            x_grouped[mt] = xg
            for half in range(2):
                nc.scalar.copy(
                    out=xg[:, 2 * half : 2 * half + 2, :, :].bitcast(F32),
                    in_=x_banks[(mt, half)][:].rearrange("p g s t -> p g t s"),
                )

        def quantize_x(mt):
            nc.vector.quantize_mx(
                out=x_codes[:, mt, :, :].rearrange("p g t -> p (g t)").bitcast(FP8X4),
                scales=x_scales[:, mt, :, :].rearrange("p g t -> p (g t)"),
                in_=x_grouped[mt][:].rearrange("p g t j -> p (g t j)"),
            )

        def store(ng, mt, res):
            o_ap, c0 = o_of[ng]
            nc.sync.dma_start(out=o_ap[mt, :, c0 : c0 + N_TILE], in_=res)

        def rotate(ng, mt):
            if mt % 2 == 0:
                prods[(ng, mt // 2)] = prod_pool.tile(
                    [P, 2, HEADS_PER_GROUP, 2 * HALF, 2], F32, name="prod", tag="prod"
                )
            shape = [P, HEADS_PER_GROUP, 2 * HALF, 2]
            nc.vector.tensor_tensor(
                out=prods[(ng, mt // 2)][:, mt % 2, :, :, :],
                in0=banks[(ng, mt)][:].to_broadcast(shape),
                in1=table[:, mt : mt + 1, :, :].to_broadcast(shape),
                op=MULT,
            )

        def result_tile(ng, mt):
            if (ng, mt // 2) not in sums:
                sums[(ng, mt // 2)] = res_pool.tile([P, 2, N_TILE], F32, name="res", tag="res")
            return sums[(ng, mt // 2)]

        def add_and_store(ng, mt, engine):
            res = result_tile(ng, mt)
            terms = prods[(ng, mt // 2)][:, mt % 2, :, :, :].rearrange("p h (i a) b -> p (h i) a b", a=2)
            engine.tensor_tensor(
                out=res[:, mt % 2, :].rearrange("p (n b) -> p n b", b=2),
                in0=terms[:, :, 0, :],
                in1=terms[:, :, 1, :],
                op=ADD,
            )
            store(ng, mt, res[:, mt % 2, :])

        def wait_for_codes(u):
            nc.gpsimd.tensor_copy(out=gate[:], in_=codes[u // PASSES][0][:, u % PASSES, 0:8])

        def add_pair_and_store(ng, half, engine):
            res = result_tile(ng, 2 * half)
            terms = prods[(ng, half)][:].rearrange("p t h (i a) b -> p (t h i) a b", a=2)
            engine.tensor_tensor(
                out=res[:].rearrange("p t (n b) -> p (t n) b", b=2),
                in0=terms[:, :, 0, :],
                in1=terms[:, :, 1, :],
                op=ADD,
            )
            store(ng, 2 * half, res[:, 0, :])
            store(ng, 2 * half + 1, res[:, 1, :])

        def copy_and_store(mt):
            res = result_tile(GROUPS - 1, mt)
            nc.scalar.copy(
                out=res[:, mt % 2, :], in_=banks[(GROUPS - 1, mt)][:].rearrange("p h c o -> p (h c o)")
            )
            store(GROUPS - 1, mt, res[:, mt % 2, :])

        all_tiles = list(range(TOKEN_TILES))

        def quantize_and_multiply(u):
            quantize(u)
            multiply(u, all_tiles)

        interleave_up_to(2)
        for mt in all_tiles:
            transpose_x(mt)
        quantize(0, 2)
        gather_x(0)
        interleave_up_to(4)
        quantize(2, 2)
        quantize_x(0)
        quantize(4)
        gather_x(1)
        interleave_up_to(5)
        quantize_x(1)
        gather_x(2)
        quantize_x(2)
        gather_x(3)
        interleave_up_to(6)
        quantize_x(3)
        quantize(5)
        for mt in all_tiles:
            for g in range(PASSES):
                multiply(g, [mt])

        for u in range(20, UNITS):
            load_unit(u)

        for c in range(GROUPS - 2):
            first = PASSES * (c + 1) + 2
            if c > 0:
                stage(first + 4)
                wait_for_codes(first - 1)
                add_pair_and_store(c - 1, 1, nc.gpsimd)
            for mt in all_tiles:
                rotate(c, mt)
                multiply(first - 2, [mt])
                multiply(first - 1, [mt])
            add_and_store(c, 0, nc.gpsimd)
            interleave_up_to(first + 1)
            quantize(first, 2)
            for mt in all_tiles:
                multiply(first, [mt])
                multiply(first + 1, [mt])
            stage(first + 6)
            interleave_up_to(first + 3 + LOOK)
            add_and_store(c, 1, nc.vector)
            quantize(first + 2, 2)

        last = GROUPS - 2
        multiply(UNITS - 4, all_tiles)
        multiply(UNITS - 3, all_tiles)
        quantize_and_multiply(UNITS - 2)
        wait_for_codes(UNITS - 2)
        add_pair_and_store(last - 1, 1, nc.gpsimd)
        rotate(last, 0)
        rotate(last, 1)
        add_and_store(last, 0, nc.vector)
        quantize_and_multiply(UNITS - 1)
        add_and_store(last, 1, nc.vector)
        rotate(last, 2)
        for mt in all_tiles:
            copy_and_store(mt)
        add_and_store(last, 2, nc.gpsimd)
        rotate(last, 3)
        add_and_store(last, 3, nc.vector)
